import numpy as np
import ml_dtypes


def mxq(x, axis, fmt="e4m3"):
    dtype, down = {"e4m3": (ml_dtypes.float8_e4m3fn, 7), "e5m2": (ml_dtypes.float8_e5m2, 14)}[fmt]
    v = np.moveaxis(np.asarray(x, np.float32).astype(ml_dtypes.bfloat16).astype(np.float64), axis, -1)
    blocks = v.reshape(v.shape[:-1] + (-1, 32))
    amax = np.abs(blocks).max(-1, keepdims=True)
    byte = np.maximum(np.where(amax > 0, np.frexp(amax)[1] - 1 + 127, 0) - down, 1)
    scale = np.exp2(byte - 127.0)
    codes = (blocks / scale).astype(np.float32).astype(dtype).astype(np.float64)
    return np.moveaxis((codes * scale).reshape(v.shape), -1, axis)


WIDE = False


def mx_kscale(k):
    if not WIDE:
        return np.ones(k)
    levels = np.array([10, -10, 5, -5, 0])
    a = np.random.permutation(np.resize(levels, k // 512 * 4)).reshape(k // 512, 4)
    idx = np.arange(k)
    return np.exp2(a[idx // 512, idx % 128 // 32])


BF16 = ml_dtypes.bfloat16


def bf(x):
    return np.asarray(x, np.float32).astype(BF16)


def f64(x):
    return np.asarray(x).astype(np.float64)


E2M1 = np.array([0.0, 0.5, 1.0, 1.5, 2.0, 3.0, 4.0, 6.0, -0.0, -0.5, -1.0, -1.5, -2.0, -3.0, -4.0, -6.0])


def pack_weight(w, fmt):
    k, n = w.shape
    w = f64(bf(w)).reshape(k // 32, 32, n)
    amax = np.abs(w).max(1)
    if fmt == "e4m3":
        byte = np.frexp(amax)[1] - 1 + 127 - 7
    else:
        mant, ex = np.frexp(amax / 6.0)
        byte = np.where(mant > 0.5, ex, ex - 1) + 127
    byte = np.clip(np.where(amax > 0, byte, 1), 1, 254)
    scaled = (w * np.exp2(127.0 - byte)[:, None, :]).reshape(k, n).astype(np.float32)
    by_word = np.ascontiguousarray(scaled.reshape(k // 512, 128, 4, n).transpose(0, 1, 3, 2))
    if fmt == "e4m3":
        words = by_word.astype(ml_dtypes.float8_e4m3fn).view(np.uint8)
    else:
        c = by_word.astype(ml_dtypes.float4_e2m1fn).view(np.uint8) & 0xF
        words = c[..., 0::2] | (c[..., 1::2] << 4)
    return np.ascontiguousarray(words), np.ascontiguousarray(byte.astype(np.uint8).reshape(k // 512, 16, n))


def unpack_weight(words, scales, fmt):
    g, p, n, _ = words.shape
    if fmt == "e4m3":
        vals = np.ascontiguousarray(words).view(ml_dtypes.float8_e4m3fn).astype(np.float64)
    else:
        nib = np.empty((g, p, n, 4), np.uint8)
        nib[..., 0::2] = words & 0xF
        nib[..., 1::2] = words >> 4
        vals = E2M1[nib]
    vals = vals * np.repeat(np.exp2(scales.astype(np.float64) - 127.0), 8, axis=1)[..., None]
    return vals.transpose(0, 1, 3, 2).reshape(g * 512, n)


N, C, D, H, W = 4, 1, 1024, 32, 32
EPS = 1e-5


def setup_inputs():
    t = np.minimum(mx_kscale(D), 1.0) ** 2
    sig0 = 0.01 * (0.5 + np.random.random_sample((C, D)))
    sig = sig0 * t
    r = np.exp2(np.round(np.log2((sig / np.sqrt(sig**2 + EPS)) / (sig0 / np.sqrt(sig0**2 + EPS)))))
    mu = np.random.standard_normal((C, D))
    z = np.random.standard_normal((N, C, D, H, W))
    x = ((z + mu[None, :, :, None, None]) * sig[None, :, :, None, None]).reshape(N, C * D, H, W)
    weight = (np.eye(D)[None] + np.random.standard_normal((C, D, D)) / np.sqrt(D)) / r[:, None, :]
    cat = np.ascontiguousarray(np.swapaxes(weight, 1, 2)).reshape(-1, D)
    words, scales = pack_weight(cat, "e4m3")
    return {"x": bf(x), "weight_words": words, "weight_scales": scales, "bias": bf(np.random.standard_normal(C * D) * 0.3)}


def reference(x, weight_words, weight_scales, bias):
    x, bias = f64(x), f64(bias)
    n, cd, h, w = x.shape
    c = C
    d = cd // c
    mean = np.mean(x, axis=(0, 2, 3), keepdims=True)
    var = np.mean(np.square(x - mean), axis=(0, 2, 3), keepdims=True)
    xn = (x - mean) / np.sqrt(var + EPS)
    xg = xn.reshape(n, c, d, h * w)
    out = unpack_weight(weight_words, weight_scales, "e4m3").reshape(C, D, D).swapaxes(1, 2)[None] @ mxq(xg, 2, "e4m3")
    return out.reshape(n, cd, h, w) + bias[None, :, None, None]

@@ -1,0 +1,220 @@
+from contextlib import ExitStack
+
+import concourse.mybir as mybir
+from concourse.masks import make_identity
+
+F32 = mybir.dt.float32
+BF16 = mybir.dt.bfloat16
+I32 = mybir.dt.int32
+U32 = mybir.dt.uint32
+U8 = mybir.dt.uint8
+FP8X4 = mybir.dt.float8_e4m3fn_x4
+ALU = mybir.AluOpType
+ACT = mybir.ActivationFunctionType
+AXIS = mybir.AxisListType
+
+P = 128
+PACK = 4
+IMAGES = 4
+CHANNELS = 1024
+PIXELS = 1024
+PASSES = CHANNELS // (P * PACK)
+SAMPLES = IMAGES * PIXELS
+EPS = 1e-5
+
+BN_CHUNK = 512
+BN_CHUNKS = SAMPLES // BN_CHUNK
+BN_WORDS = 6
+VECTOR_T = (0, 1)
+SCALAR_T = (2, 3)
+SUM_COLS = 256
+
+N_TILE = 512
+TILES = IMAGES * PIXELS // N_TILE
+TILES_PER_IMAGE = PIXELS // N_TILE
+O_TILES = CHANNELS // P
+RUN = 4
+
+FLOPS = 2 * CHANNELS * CHANNELS * IMAGES * PIXELS
+
+
+def tile_caps_bn_t_e_kernel(tc, x, weight_words, weight_scales, bias, out):
+    nc = tc.nc
+    x_view = x.rearrange("n (g p t) h w -> n g p t (h w)", g=PASSES, p=P, t=PACK)
+    out_view = out.rearrange("n (o m) h w -> n o m (h w)", m=P)
+
+    with ExitStack() as pools:
+        const = pools.enter_context(tc.tile_pool(name="const", bufs=1))
+        x_pool = pools.enter_context(tc.tile_pool(name="x_pool", bufs=1))
+        stat = pools.enter_context(tc.tile_pool(name="stat", bufs=1))
+        scratch = pools.enter_context(tc.tile_pool(name="scratch", bufs=4))
+        work = pools.enter_context(tc.tile_pool(name="work", bufs=3))
+        quant = pools.enter_context(tc.tile_pool(name="quant", bufs=6))
+        results = pools.enter_context(tc.tile_pool(name="results", bufs=8))
+
+        one_col = const.tile([P, 1], F32, name="one_col")
+        nc.vector.memset(one_col[:], 1.0)
+        table_warm = const.tile([P, 1], F32, name="table_warm")
+        nc.scalar.activation(out=table_warm[:], in_=one_col[:], func=ACT.Sqrt)
+
+        ident = const.tile([P, P], BF16, name="ident")
+        make_identity(nc, ident[:])
+
+        w_planes = const.tile([P, PASSES, CHANNELS], U8, name="w_planes", align_bytes=64)
+        nc.vector.memset(w_planes[:].bitcast(I32), 0)
+        bias_rows = const.tile([P, P], BF16, name="bias_rows")
+        nc.vector.memset(bias_rows[:], 0.0)
+
+        x_sb = [[None] * IMAGES for g in range(PASSES)]
+        for g in range(PASSES):
+            for n in range(IMAGES):
+                x_sb[g][n] = x_pool.tile([P, PACK, PIXELS], BF16, name="x_%d_%d" % (g, n))
+                nc.sync.dma_start(out=x_sb[g][n][:], in_=x_view[n, g])
+        w_words = const.tile([P, PASSES, CHANNELS], U32, name="w_words", align_bytes=64)
+        for g in range(PASSES):
+            nc.sync.dma_start(
+                out=w_words[:, g, :].bitcast(I32),
+                in_=weight_words[g].rearrange("p n t -> p (n t)").bitcast(I32),
+            )
+        for quadrant in range(4):
+            nc.sync.dma_start(
+                out=w_planes[32 * quadrant : 32 * quadrant + 4, :, :].bitcast(I32),
+                in_=weight_scales[:, 4 * quadrant : 4 * quadrant + 4, :].bitcast(I32).rearrange("g r n -> r g n"),
+            )
+        nc.sync.dma_start(out=bias_rows[0:O_TILES, :], in_=bias.rearrange("(o m) -> o m", m=P))
+
+        mean_var = [stat.tile([P, PACK, 2], F32, name="mean_var_%d" % g) for g in range(PASSES)]
+        rstd = [stat.tile([P, PACK], F32, name="rstd_%d" % g) for g in range(PASSES)]
+        bias_col = const.tile([P, O_TILES], F32, name="bias_col")
+
+        with tc.psum_pool(name="stat_banks", bufs=1) as stat_banks:
+            for g in range(PASSES):
+                bn_out = stat.tile([P, len(VECTOR_T), BN_CHUNKS, BN_WORDS], F32, name="bn_out_%d" % g)
+                neg_shift = stat.tile([P, len(SCALAR_T)], F32, name="neg_shift_%d" % g)
+                nc.scalar.mul(out=neg_shift[:], in_=x_sb[g][0][:, SCALAR_T[0] : SCALAR_T[-1] + 1, 0], mul=-1.0)
+                squares = stat.tile([P, len(SCALAR_T), IMAGES], F32, name="squares_%d" % g)
+                sum_banks = [
+                    stat_banks.tile([P, SUM_COLS], F32, name="sum_bank_%d_%d" % (g, s)) for s in range(len(SCALAR_T))
+                ]
+                for n in range(IMAGES):
+                    for s, t in enumerate(VECTOR_T):
+                        for c in range(PIXELS // BN_CHUNK):
+                            nc.vector.bn_stats(
+                                out=bn_out[:, s, n * (PIXELS // BN_CHUNK) + c, :],
+                                in_=x_sb[g][n][:, t, c * BN_CHUNK : (c + 1) * BN_CHUNK],
+                            )
+                    for s, t in enumerate(SCALAR_T):
+                        unread = scratch.tile([P, PIXELS], BF16, name="unread")
+                        nc.scalar.activation(
+                            out=unread[:],
+                            in_=x_sb[g][n][:, t, :],
+                            func=ACT.Square,
+                            bias=neg_shift[:, s : s + 1],
+                            scale=1.0,
+                            accum_out=squares[:, s, n : n + 1],
+                        )
+                        for c in range(PIXELS // SUM_COLS):
+                            nc.tensor.matmul(
+                                out=sum_banks[s][:],
+                                lhsT=ident[:],
+                                rhs=x_sb[g][n][:, t, c * SUM_COLS : (c + 1) * SUM_COLS],
+                                start=(n == 0 and c == 0),
+                                stop=(n == IMAGES - 1 and c == PIXELS // SUM_COLS - 1),
+                            )
+
+                for s, t in enumerate(VECTOR_T):
+                    nc.vector.bn_aggr(out=mean_var[g][:, t, :], in_=bn_out[:, s].rearrange("p c w -> p (c w)"))
+                sums = stat.tile([P, len(SCALAR_T)], F32, name="sums_%d" % g)
+                for s in range(len(SCALAR_T)):
+                    nc.vector.tensor_reduce(out=sums[:, s : s + 1], in_=sum_banks[s][:], axis=AXIS.X, op=ALU.add)
+                square_sums = stat.tile([P, len(SCALAR_T)], F32, name="square_sums_%d" % g)
+                nc.vector.tensor_reduce(out=square_sums[:], in_=squares[:], axis=AXIS.X, op=ALU.add)
+                scalar_ts = slice(SCALAR_T[0], SCALAR_T[-1] + 1)
+                nc.vector.tensor_scalar_mul(out=mean_var[g][:, scalar_ts, 0], in0=sums[:], scalar1=1.0 / SAMPLES)
+                offset = stat.tile([P, len(SCALAR_T)], F32, name="offset_%d" % g)
+                nc.vector.scalar_tensor_tensor(
+                    out=offset[:], in0=sums[:], scalar=1.0 / SAMPLES, in1=neg_shift[:], op0=ALU.mult, op1=ALU.add
+                )
+                offset_sq = stat.tile([P, len(SCALAR_T)], F32, name="offset_sq_%d" % g)
+                nc.vector.tensor_mul(out=offset_sq[:], in0=offset[:], in1=offset[:])
+                nc.vector.scalar_tensor_tensor(
+                    out=mean_var[g][:, scalar_ts, 1],
+                    in0=square_sums[:],
+                    scalar=1.0 / SAMPLES,
+                    in1=offset_sq[:],
+                    op0=ALU.mult,
+                    op1=ALU.subtract,
+                )
+                std = stat.tile([P, PACK], F32, name="std_%d" % g)
+                nc.scalar.activation(out=std[:], in_=mean_var[g][:, :, 1], func=ACT.Sqrt, bias=EPS, scale=1.0)
+                nc.vector.reciprocal(out=rstd[g][:], in_=std[:])
+
+            bias_ps = stat_banks.tile([P, P], BF16, name="bias_ps")
+            nc.tensor.transpose(bias_ps[:], bias_rows[:], ident[:])
+            nc.vector.tensor_copy(out=bias_col[:], in_=bias_ps[:, 0:O_TILES])
+
+        def normalise(j, g):
+            n, half = divmod(j, TILES_PER_IMAGE)
+            xn = work.tile([P, PACK, N_TILE], BF16, name="xn")
+            for t in range(PACK):
+                nc.vector.tensor_scalar(
+                    out=xn[:, t, :],
+                    in0=x_sb[g][n][:, t, half * N_TILE : (half + 1) * N_TILE],
+                    scalar1=mean_var[g][:, t, 0:1],
+                    scalar2=rstd[g][:, t : t + 1],
+                    op0=ALU.subtract,
+                    op1=ALU.mult,
+                )
+            return xn
+
+        def regroup(xn):
+            grouped = work.tile([P, N_TILE, PACK], BF16, name="grouped", align_bytes=64)
+            nc.vector.tensor_copy(
+                out=grouped[:].rearrange("p (c i) t -> p c t i", i=RUN),
+                in_=xn[:].rearrange("p t (c i) -> p c t i", i=RUN),
+            )
+            return grouped
+
+        def quantise(grouped):
+            codes = quant.tile([P, N_TILE], U32, name="codes", align_bytes=64)
+            plane = quant.tile([P, N_TILE], U8, name="plane", align_bytes=64)
+            nc.vector.quantize_mx(
+                out=codes[:].bitcast(FP8X4), scales=plane[:], in_=grouped[:].rearrange("p c t -> p (c t)")
+            )
+            return codes, plane
+
+        with tc.psum_pool(name="acc_banks", bufs=8) as acc_banks:
+
+            def multiply_and_store(j, operands):
+                n, half = divmod(j, TILES_PER_IMAGE)
+                for o in range(O_TILES):
+                    o_cols = slice(o * P, (o + 1) * P)
+                    acc = acc_banks.tile([P, N_TILE], F32, name="acc")
+                    for g in range(PASSES):
+                        codes, plane = operands[g]
+                        nc.tensor.matmul_mx(
+                            out=acc[:],
+                            lhsT=w_words[:, g, o_cols].bitcast(FP8X4),
+                            lhsT_scale=w_planes[:, g, o_cols],
+                            rhs=codes[:].bitcast(FP8X4),
+                            rhs_scale=plane[:],
+                            start=(g == 0),
+                            stop=(g == PASSES - 1),
+                        )
+                    result = results.tile([P, N_TILE], F32, name="result")
+                    nc.scalar.activation(
+                        out=result[:], in_=acc[:], func=ACT.Identity, bias=bias_col[:, o : o + 1], scale=1.0
+                    )
+                    nc.sync.dma_start(out=out_view[n, o][:, half * N_TILE : (half + 1) * N_TILE], in_=result[:])
+
+            units = [(j, g) for j in range(TILES) for g in range(PASSES)]
+            xn_next = normalise(*units[0])
+            operands = []
+            for u, (j, g) in enumerate(units):
+                grouped = regroup(xn_next)
+                if u + 1 < len(units):
+                    xn_next = normalise(*units[u + 1])
+                operands.append(quantise(grouped))
+                if g == PASSES - 1:
+                    multiply_and_store(j, operands)
+                    operands = []

@@ -22,25 +22,36 @@ PASSES = CHANNELS // (P * PACK)
 SAMPLES = IMAGES * PIXELS
 EPS = 1e-5
 
+HALF = PACK // 2
+BY_VECTOR = 0
+BY_SCALAR = 1
 BN_CHUNK = 512
-BN_CHUNKS = SAMPLES // BN_CHUNK
+BN_PER_IMAGE = PIXELS // BN_CHUNK
 BN_WORDS = 6
-VECTOR_T = (0, 1)
-SCALAR_T = (2, 3)
 SUM_COLS = 256
 
 N_TILE = 512
-TILES = IMAGES * PIXELS // N_TILE
-TILES_PER_IMAGE = PIXELS // N_TILE
+FIRST_TILE = 128
 O_TILES = CHANNELS // P
 RUN = 4
 
 FLOPS = 2 * CHANNELS * CHANNELS * IMAGES * PIXELS
 
 
+def pixel_tiles():
+    tiles = []
+    first = 0
+    width = FIRST_TILE
+    while first < IMAGES * PIXELS:
+        tiles.append((first, width))
+        first += width
+        width = min(first, N_TILE)
+    return tiles
+
+
 def tile_caps_bn_t_e_kernel(tc, x, weight_words, weight_scales, bias, out):
     nc = tc.nc
-    x_view = x.rearrange("n (g p t) h w -> n g p t (h w)", g=PASSES, p=P, t=PACK)
+    x_view = x.rearrange("n (g p a b) h w -> n g a p b (h w)", g=PASSES, p=P, a=PACK // HALF, b=HALF)
     out_view = out.rearrange("n (o m) h w -> n o m (h w)", m=P)
 
     with ExitStack() as pools:
@@ -48,9 +59,9 @@ def tile_caps_bn_t_e_kernel(tc, x, weight_words, weight_scales, bias, out):
         x_pool = pools.enter_context(tc.tile_pool(name="x_pool", bufs=1))
         stat = pools.enter_context(tc.tile_pool(name="stat", bufs=1))
         scratch = pools.enter_context(tc.tile_pool(name="scratch", bufs=4))
-        work = pools.enter_context(tc.tile_pool(name="work", bufs=3))
-        quant = pools.enter_context(tc.tile_pool(name="quant", bufs=6))
-        results = pools.enter_context(tc.tile_pool(name="results", bufs=8))
+        work = pools.enter_context(tc.tile_pool(name="work", bufs=4))
+        quant = pools.enter_context(tc.tile_pool(name="quant", bufs=8))
+        results = pools.enter_context(tc.tile_pool(name="results", bufs=12))
 
         one_col = const.tile([P, 1], F32, name="one_col")
         nc.vector.memset(one_col[:], 1.0)
@@ -65,11 +76,12 @@ def tile_caps_bn_t_e_kernel(tc, x, weight_words, weight_scales, bias, out):
         bias_rows = const.tile([P, P], BF16, name="bias_rows")
         nc.vector.memset(bias_rows[:], 0.0)
 
-        x_sb = [[None] * IMAGES for g in range(PASSES)]
+        x_sb = [[[None, None] for n in range(IMAGES)] for g in range(PASSES)]
         for g in range(PASSES):
             for n in range(IMAGES):
-                x_sb[g][n] = x_pool.tile([P, PACK, PIXELS], BF16, name="x_%d_%d" % (g, n))
-                nc.sync.dma_start(out=x_sb[g][n][:], in_=x_view[n, g])
+                for a in (BY_SCALAR, BY_VECTOR):
+                    x_sb[g][n][a] = x_pool.tile([P, HALF, PIXELS], BF16, name="x_%d_%d_%d" % (g, n, a))
+                    nc.sync.dma_start(out=x_sb[g][n][a][:], in_=x_view[n, g, a])
         w_words = const.tile([P, PASSES, CHANNELS], U32, name="w_words", align_bytes=64)
         for g in range(PASSES):
             nc.sync.dma_start(
@@ -86,57 +98,57 @@ def tile_caps_bn_t_e_kernel(tc, x, weight_words, weight_scales, bias, out):
         mean_var = [stat.tile([P, PACK, 2], F32, name="mean_var_%d" % g) for g in range(PASSES)]
         rstd = [stat.tile([P, PACK], F32, name="rstd_%d" % g) for g in range(PASSES)]
         bias_col = const.tile([P, O_TILES], F32, name="bias_col")
+        scalar_ts = slice(BY_SCALAR * HALF, (BY_SCALAR + 1) * HALF)
 
         with tc.psum_pool(name="stat_banks", bufs=1) as stat_banks:
             for g in range(PASSES):
-                bn_out = stat.tile([P, len(VECTOR_T), BN_CHUNKS, BN_WORDS], F32, name="bn_out_%d" % g)
-                neg_shift = stat.tile([P, len(SCALAR_T)], F32, name="neg_shift_%d" % g)
-                nc.scalar.mul(out=neg_shift[:], in_=x_sb[g][0][:, SCALAR_T[0] : SCALAR_T[-1] + 1, 0], mul=-1.0)
-                squares = stat.tile([P, len(SCALAR_T), IMAGES], F32, name="squares_%d" % g)
-                sum_banks = [
-                    stat_banks.tile([P, SUM_COLS], F32, name="sum_bank_%d_%d" % (g, s)) for s in range(len(SCALAR_T))
-                ]
+                bn_out = stat.tile([P, HALF, IMAGES * BN_PER_IMAGE, BN_WORDS], F32, name="bn_out_%d" % g)
+                neg_shift = stat.tile([P, HALF], F32, name="neg_shift_%d" % g)
+                nc.scalar.mul(out=neg_shift[:], in_=x_sb[g][0][BY_SCALAR][:, :, 0], mul=-1.0)
+                squares = stat.tile([P, HALF, IMAGES], F32, name="squares_%d" % g)
+                sum_banks = [stat_banks.tile([P, SUM_COLS], F32, name="sum_bank_%d_%d" % (g, b)) for b in range(HALF)]
                 for n in range(IMAGES):
-                    for s, t in enumerate(VECTOR_T):
-                        for c in range(PIXELS // BN_CHUNK):
-                            nc.vector.bn_stats(
-                                out=bn_out[:, s, n * (PIXELS // BN_CHUNK) + c, :],
-                                in_=x_sb[g][n][:, t, c * BN_CHUNK : (c + 1) * BN_CHUNK],
-                            )
-                    for s, t in enumerate(SCALAR_T):
+                    for b in range(HALF):
                         unread = scratch.tile([P, PIXELS], BF16, name="unread")
                         nc.scalar.activation(
                             out=unread[:],
-                            in_=x_sb[g][n][:, t, :],
+                            in_=x_sb[g][n][BY_SCALAR][:, b, :],
                             func=ACT.Square,
-                            bias=neg_shift[:, s : s + 1],
+                            bias=neg_shift[:, b : b + 1],
                             scale=1.0,
-                            accum_out=squares[:, s, n : n + 1],
+                            accum_out=squares[:, b, n : n + 1],
                         )
                         for c in range(PIXELS // SUM_COLS):
                             nc.tensor.matmul(
-                                out=sum_banks[s][:],
+                                out=sum_banks[b][:],
                                 lhsT=ident[:],
-                                rhs=x_sb[g][n][:, t, c * SUM_COLS : (c + 1) * SUM_COLS],
+                                rhs=x_sb[g][n][BY_SCALAR][:, b, c * SUM_COLS : (c + 1) * SUM_COLS],
                                 start=(n == 0 and c == 0),
                                 stop=(n == IMAGES - 1 and c == PIXELS // SUM_COLS - 1),
                             )
+                    for b in range(HALF):
+                        for c in range(BN_PER_IMAGE):
+                            nc.vector.bn_stats(
+                                out=bn_out[:, b, n * BN_PER_IMAGE + c, :],
+                                in_=x_sb[g][n][BY_VECTOR][:, b, c * BN_CHUNK : (c + 1) * BN_CHUNK],
+                            )
 
-                for s, t in enumerate(VECTOR_T):
-                    nc.vector.bn_aggr(out=mean_var[g][:, t, :], in_=bn_out[:, s].rearrange("p c w -> p (c w)"))
-                sums = stat.tile([P, len(SCALAR_T)], F32, name="sums_%d" % g)
-                for s in range(len(SCALAR_T)):
-                    nc.vector.tensor_reduce(out=sums[:, s : s + 1], in_=sum_banks[s][:], axis=AXIS.X, op=ALU.add)
-                square_sums = stat.tile([P, len(SCALAR_T)], F32, name="square_sums_%d" % g)
-                nc.vector.tensor_reduce(out=square_sums[:], in_=squares[:], axis=AXIS.X, op=ALU.add)
-                scalar_ts = slice(SCALAR_T[0], SCALAR_T[-1] + 1)
+                for b in range(HALF):
+                    nc.vector.bn_aggr(
+                        out=mean_var[g][:, BY_VECTOR * HALF + b, :], in_=bn_out[:, b].rearrange("p c w -> p (c w)")
+                    )
+                sums = stat.tile([P, HALF], F32, name="sums_%d" % g)
+                for b in range(HALF):
+                    nc.vector.tensor_reduce(out=sums[:, b : b + 1], in_=sum_banks[b][:], axis=AXIS.X, op=ALU.add)
                 nc.vector.tensor_scalar_mul(out=mean_var[g][:, scalar_ts, 0], in0=sums[:], scalar1=1.0 / SAMPLES)
-                offset = stat.tile([P, len(SCALAR_T)], F32, name="offset_%d" % g)
+                offset = stat.tile([P, HALF], F32, name="offset_%d" % g)
                 nc.vector.scalar_tensor_tensor(
                     out=offset[:], in0=sums[:], scalar=1.0 / SAMPLES, in1=neg_shift[:], op0=ALU.mult, op1=ALU.add
                 )
-                offset_sq = stat.tile([P, len(SCALAR_T)], F32, name="offset_sq_%d" % g)
+                offset_sq = stat.tile([P, HALF], F32, name="offset_sq_%d" % g)
                 nc.vector.tensor_mul(out=offset_sq[:], in0=offset[:], in1=offset[:])
+                square_sums = stat.tile([P, HALF], F32, name="square_sums_%d" % g)
+                nc.vector.tensor_reduce(out=square_sums[:], in_=squares[:], axis=AXIS.X, op=ALU.add)
                 nc.vector.scalar_tensor_tensor(
                     out=mean_var[g][:, scalar_ts, 1],
                     in0=square_sums[:],
@@ -153,13 +165,13 @@ def tile_caps_bn_t_e_kernel(tc, x, weight_words, weight_scales, bias, out):
             nc.tensor.transpose(bias_ps[:], bias_rows[:], ident[:])
             nc.vector.tensor_copy(out=bias_col[:], in_=bias_ps[:, 0:O_TILES])
 
-        def normalise(j, g):
-            n, half = divmod(j, TILES_PER_IMAGE)
+        def normalise(first, width, g):
+            n, col = divmod(first, PIXELS)
             xn = work.tile([P, PACK, N_TILE], BF16, name="xn")
             for t in range(PACK):
                 nc.vector.tensor_scalar(
-                    out=xn[:, t, :],
-                    in0=x_sb[g][n][:, t, half * N_TILE : (half + 1) * N_TILE],
+                    out=xn[:, t, :width],
+                    in0=x_sb[g][n][t // HALF][:, t % HALF, col : col + width],
                     scalar1=mean_var[g][:, t, 0:1],
                     scalar2=rstd[g][:, t : t + 1],
                     op0=ALU.subtract,
@@ -167,54 +179,57 @@ def tile_caps_bn_t_e_kernel(tc, x, weight_words, weight_scales, bias, out):
                 )
             return xn
 
-        def regroup(xn):
+        def regroup(xn, width):
             grouped = work.tile([P, N_TILE, PACK], BF16, name="grouped", align_bytes=64)
             nc.vector.tensor_copy(
-                out=grouped[:].rearrange("p (c i) t -> p c t i", i=RUN),
-                in_=xn[:].rearrange("p t (c i) -> p c t i", i=RUN),
+                out=grouped[:, :width, :].rearrange("p (c i) t -> p c t i", i=RUN),
+                in_=xn[:, :, :width].rearrange("p t (c i) -> p c t i", i=RUN),
             )
             return grouped
 
-        def quantise(grouped):
+        def quantise(grouped, width):
             codes = quant.tile([P, N_TILE], U32, name="codes", align_bytes=64)
             plane = quant.tile([P, N_TILE], U8, name="plane", align_bytes=64)
             nc.vector.quantize_mx(
-                out=codes[:].bitcast(FP8X4), scales=plane[:], in_=grouped[:].rearrange("p c t -> p (c t)")
+                out=codes[:, :width].bitcast(FP8X4),
+                scales=plane[:, :width],
+                in_=grouped[:, :width, :].rearrange("p c t -> p (c t)"),
             )
             return codes, plane
 
-        with tc.psum_pool(name="acc_banks", bufs=8) as acc_banks:
+        with tc.psum_pool(name="acc_banks", bufs=O_TILES) as acc_banks:
 
-            def multiply_and_store(j, operands):
-                n, half = divmod(j, TILES_PER_IMAGE)
-                for o in range(O_TILES):
-                    o_cols = slice(o * P, (o + 1) * P)
-                    acc = acc_banks.tile([P, N_TILE], F32, name="acc")
-                    for g in range(PASSES):
-                        codes, plane = operands[g]
-                        nc.tensor.matmul_mx(
-                            out=acc[:],
-                            lhsT=w_words[:, g, o_cols].bitcast(FP8X4),
-                            lhsT_scale=w_planes[:, g, o_cols],
-                            rhs=codes[:].bitcast(FP8X4),
-                            rhs_scale=plane[:],
-                            start=(g == 0),
-                            stop=(g == PASSES - 1),
-                        )
-                    result = results.tile([P, N_TILE], F32, name="result")
-                    nc.scalar.activation(
-                        out=result[:], in_=acc[:], func=ACT.Identity, bias=bias_col[:, o : o + 1], scale=1.0
-                    )
-                    nc.sync.dma_start(out=out_view[n, o][:, half * N_TILE : (half + 1) * N_TILE], in_=result[:])
+            def multiply(acc, o, g, codes, plane, width):
+                o_cols = slice(o * P, (o + 1) * P)
+                nc.tensor.matmul_mx(
+                    out=acc[:, :width],
+                    lhsT=w_words[:, g, o_cols].bitcast(FP8X4),
+                    lhsT_scale=w_planes[:, g, o_cols],
+                    rhs=codes[:, :width].bitcast(FP8X4),
+                    rhs_scale=plane[:, :width],
+                    start=(g == 0),
+                    stop=(g == PASSES - 1),
+                )
 
-            units = [(j, g) for j in range(TILES) for g in range(PASSES)]
+            def add_bias_and_store(acc, o, first, width):
+                n, col = divmod(first, PIXELS)
+                result = results.tile([P, N_TILE], F32, name="result")
+                nc.scalar.activation(
+                    out=result[:, :width], in_=acc[:, :width], func=ACT.Identity, bias=bias_col[:, o : o + 1], scale=1.0
+                )
+                nc.sync.dma_start(out=out_view[n, o][:, col : col + width], in_=result[:, :width])
+
+            units = [(first, width, g) for first, width in pixel_tiles() for g in range(PASSES)]
             xn_next = normalise(*units[0])
-            operands = []
-            for u, (j, g) in enumerate(units):
-                grouped = regroup(xn_next)
+            accs = []
+            for u, (first, width, g) in enumerate(units):
+                grouped = regroup(xn_next, width)
                 if u + 1 < len(units):
                     xn_next = normalise(*units[u + 1])
-                operands.append(quantise(grouped))
-                if g == PASSES - 1:
-                    multiply_and_store(j, operands)
-                    operands = []
+                codes, plane = quantise(grouped, width)
+                if g == 0:
+                    accs = [acc_banks.tile([P, N_TILE], F32, name="acc") for o in range(O_TILES)]
+                for o in range(O_TILES):
+                    multiply(accs[o], o, g, codes, plane, width)
+                    if g == PASSES - 1:
+                        add_bias_and_store(accs[o], o, first, width)

@@ -28,7 +28,7 @@ BY_SCALAR = 1
 BN_CHUNK = 512
 BN_PER_IMAGE = PIXELS // BN_CHUNK
 BN_WORDS = 6
-SUM_COLS = 256
+SUM_COLS = 128
 
 N_TILE = 512
 FIRST_TILE = 128
@@ -59,6 +59,7 @@ def tile_caps_bn_t_e_kernel(tc, x, weight_words, weight_scales, bias, out):
         x_pool = pools.enter_context(tc.tile_pool(name="x_pool", bufs=1))
         stat = pools.enter_context(tc.tile_pool(name="stat", bufs=1))
         scratch = pools.enter_context(tc.tile_pool(name="scratch", bufs=4))
+        images = pools.enter_context(tc.tile_pool(name="images", bufs=4))
         work = pools.enter_context(tc.tile_pool(name="work", bufs=4))
         quant = pools.enter_context(tc.tile_pool(name="quant", bufs=8))
         results = pools.enter_context(tc.tile_pool(name="results", bufs=12))
@@ -79,7 +80,7 @@ def tile_caps_bn_t_e_kernel(tc, x, weight_words, weight_scales, bias, out):
         x_sb = [[[None, None] for n in range(IMAGES)] for g in range(PASSES)]
         for g in range(PASSES):
             for n in range(IMAGES):
-                for a in (BY_SCALAR, BY_VECTOR):
+                for a in (BY_VECTOR, BY_SCALAR):
                     x_sb[g][n][a] = x_pool.tile([P, HALF, PIXELS], BF16, name="x_%d_%d_%d" % (g, n, a))
                     nc.sync.dma_start(out=x_sb[g][n][a][:], in_=x_view[n, g, a])
         w_words = const.tile([P, PASSES, CHANNELS], U32, name="w_words", align_bytes=64)
@@ -95,95 +96,95 @@ def tile_caps_bn_t_e_kernel(tc, x, weight_words, weight_scales, bias, out):
             )
         nc.sync.dma_start(out=bias_rows[0:O_TILES, :], in_=bias.rearrange("(o m) -> o m", m=P))
 
-        mean_var = [stat.tile([P, PACK, 2], F32, name="mean_var_%d" % g) for g in range(PASSES)]
-        rstd = [stat.tile([P, PACK], F32, name="rstd_%d" % g) for g in range(PASSES)]
+        mean_var = stat.tile([P, PASSES, PACK, 2], F32, name="mean_var")
+        rstd = stat.tile([P, PASSES, PACK], F32, name="rstd")
         bias_col = const.tile([P, O_TILES], F32, name="bias_col")
         scalar_ts = slice(BY_SCALAR * HALF, (BY_SCALAR + 1) * HALF)
 
+        bn_out = stat.tile([P, PASSES, HALF, IMAGES * BN_PER_IMAGE, BN_WORDS], F32, name="bn_out")
+        neg_shift = stat.tile([P, PASSES, HALF], F32, name="neg_shift")
+        squares = stat.tile([P, PASSES, HALF, IMAGES], F32, name="squares")
         with tc.psum_pool(name="stat_banks", bufs=1) as stat_banks:
+            sum_banks = [stat_banks.tile([P, HALF, SUM_COLS], F32, name="sum_bank_%d" % g) for g in range(PASSES)]
             for g in range(PASSES):
-                bn_out = stat.tile([P, HALF, IMAGES * BN_PER_IMAGE, BN_WORDS], F32, name="bn_out_%d" % g)
-                neg_shift = stat.tile([P, HALF], F32, name="neg_shift_%d" % g)
-                nc.scalar.mul(out=neg_shift[:], in_=x_sb[g][0][BY_SCALAR][:, :, 0], mul=-1.0)
-                squares = stat.tile([P, HALF, IMAGES], F32, name="squares_%d" % g)
-                sum_banks = [stat_banks.tile([P, SUM_COLS], F32, name="sum_bank_%d_%d" % (g, b)) for b in range(HALF)]
+                nc.scalar.mul(out=neg_shift[:, g, :], in_=x_sb[g][0][BY_SCALAR][:, :, 0], mul=-1.0)
                 for n in range(IMAGES):
+                    for b in range(HALF):
+                        for c in range(BN_PER_IMAGE):
+                            nc.vector.bn_stats(
+                                out=bn_out[:, g, b, n * BN_PER_IMAGE + c, :],
+                                in_=x_sb[g][n][BY_VECTOR][:, b, c * BN_CHUNK : (c + 1) * BN_CHUNK],
+                            )
                     for b in range(HALF):
                         unread = scratch.tile([P, PIXELS], BF16, name="unread")
                         nc.scalar.activation(
                             out=unread[:],
                             in_=x_sb[g][n][BY_SCALAR][:, b, :],
                             func=ACT.Square,
-                            bias=neg_shift[:, b : b + 1],
+                            bias=neg_shift[:, g, b : b + 1],
                             scale=1.0,
-                            accum_out=squares[:, b, n : n + 1],
+                            accum_out=squares[:, g, b, n : n + 1],
                         )
-                        for c in range(PIXELS // SUM_COLS):
-                            nc.tensor.matmul(
-                                out=sum_banks[b][:],
-                                lhsT=ident[:],
-                                rhs=x_sb[g][n][BY_SCALAR][:, b, c * SUM_COLS : (c + 1) * SUM_COLS],
-                                start=(n == 0 and c == 0),
-                                stop=(n == IMAGES - 1 and c == PIXELS // SUM_COLS - 1),
-                            )
-                    for b in range(HALF):
-                        for c in range(BN_PER_IMAGE):
-                            nc.vector.bn_stats(
-                                out=bn_out[:, b, n * BN_PER_IMAGE + c, :],
-                                in_=x_sb[g][n][BY_VECTOR][:, b, c * BN_CHUNK : (c + 1) * BN_CHUNK],
-                            )
+                    for c in range(PIXELS // SUM_COLS):
+                        nc.tensor.matmul(
+                            out=sum_banks[g][:],
+                            lhsT=ident[:],
+                            rhs=x_sb[g][n][BY_SCALAR][:, :, c * SUM_COLS : (c + 1) * SUM_COLS],
+                            start=(n == 0 and c == 0),
+                            stop=(n == IMAGES - 1 and c == PIXELS // SUM_COLS - 1),
+                        )
 
+            for g in range(PASSES):
                 for b in range(HALF):
                     nc.vector.bn_aggr(
-                        out=mean_var[g][:, BY_VECTOR * HALF + b, :], in_=bn_out[:, b].rearrange("p c w -> p (c w)")
+                        out=mean_var[:, g, BY_VECTOR * HALF + b, :], in_=bn_out[:, g, b].rearrange("p c w -> p (c w)")
                     )
-                sums = stat.tile([P, HALF], F32, name="sums_%d" % g)
-                for b in range(HALF):
-                    nc.vector.tensor_reduce(out=sums[:, b : b + 1], in_=sum_banks[b][:], axis=AXIS.X, op=ALU.add)
-                nc.vector.tensor_scalar_mul(out=mean_var[g][:, scalar_ts, 0], in0=sums[:], scalar1=1.0 / SAMPLES)
-                offset = stat.tile([P, HALF], F32, name="offset_%d" % g)
-                nc.vector.scalar_tensor_tensor(
-                    out=offset[:], in0=sums[:], scalar=1.0 / SAMPLES, in1=neg_shift[:], op0=ALU.mult, op1=ALU.add
-                )
-                offset_sq = stat.tile([P, HALF], F32, name="offset_sq_%d" % g)
-                nc.vector.tensor_mul(out=offset_sq[:], in0=offset[:], in1=offset[:])
-                square_sums = stat.tile([P, HALF], F32, name="square_sums_%d" % g)
-                nc.vector.tensor_reduce(out=square_sums[:], in_=squares[:], axis=AXIS.X, op=ALU.add)
-                nc.vector.scalar_tensor_tensor(
-                    out=mean_var[g][:, scalar_ts, 1],
-                    in0=square_sums[:],
-                    scalar=1.0 / SAMPLES,
-                    in1=offset_sq[:],
-                    op0=ALU.mult,
-                    op1=ALU.subtract,
-                )
-                std = stat.tile([P, PACK], F32, name="std_%d" % g)
-                nc.scalar.activation(out=std[:], in_=mean_var[g][:, :, 1], func=ACT.Sqrt, bias=EPS, scale=1.0)
-                nc.vector.reciprocal(out=rstd[g][:], in_=std[:])
+            sums = stat.tile([P, PASSES, HALF], F32, name="sums")
+            for g in range(PASSES):
+                nc.vector.tensor_reduce(out=sums[:, g, :], in_=sum_banks[g][:], axis=AXIS.X, op=ALU.add)
+            nc.vector.tensor_scalar_mul(out=mean_var[:, :, scalar_ts, 0], in0=sums[:], scalar1=1.0 / SAMPLES)
+            offset = stat.tile([P, PASSES, HALF], F32, name="offset")
+            nc.vector.scalar_tensor_tensor(
+                out=offset[:], in0=sums[:], scalar=1.0 / SAMPLES, in1=neg_shift[:], op0=ALU.mult, op1=ALU.add
+            )
+            offset_sq = stat.tile([P, PASSES, HALF], F32, name="offset_sq")
+            nc.vector.tensor_mul(out=offset_sq[:], in0=offset[:], in1=offset[:])
+            square_sums = stat.tile([P, PASSES, HALF], F32, name="square_sums")
+            nc.vector.tensor_reduce(out=square_sums[:], in_=squares[:], axis=AXIS.X, op=ALU.add)
+            nc.vector.scalar_tensor_tensor(
+                out=mean_var[:, :, scalar_ts, 1],
+                in0=square_sums[:],
+                scalar=1.0 / SAMPLES,
+                in1=offset_sq[:],
+                op0=ALU.mult,
+                op1=ALU.subtract,
+            )
+            std = stat.tile([P, PASSES, PACK], F32, name="std")
+            nc.scalar.activation(out=std[:], in_=mean_var[:, :, :, 1], func=ACT.Sqrt, bias=EPS, scale=1.0)
+            nc.vector.reciprocal(out=rstd[:], in_=std[:])
 
             bias_ps = stat_banks.tile([P, P], BF16, name="bias_ps")
             nc.tensor.transpose(bias_ps[:], bias_rows[:], ident[:])
             nc.vector.tensor_copy(out=bias_col[:], in_=bias_ps[:, 0:O_TILES])
 
-        def normalise(first, width, g):
-            n, col = divmod(first, PIXELS)
-            xn = work.tile([P, PACK, N_TILE], BF16, name="xn")
+        def normalise(n, g):
+            xn = images.tile([P, PACK, PIXELS], BF16, name="xn")
             for t in range(PACK):
                 nc.vector.tensor_scalar(
-                    out=xn[:, t, :width],
-                    in0=x_sb[g][n][t // HALF][:, t % HALF, col : col + width],
-                    scalar1=mean_var[g][:, t, 0:1],
-                    scalar2=rstd[g][:, t : t + 1],
+                    out=xn[:, t, :],
+                    in0=x_sb[g][n][t // HALF][:, t % HALF, :],
+                    scalar1=mean_var[:, g, t, 0:1],
+                    scalar2=rstd[:, g, t : t + 1],
                     op0=ALU.subtract,
                     op1=ALU.mult,
                 )
             return xn
 
-        def regroup(xn, width):
+        def regroup(xn, col, width):
             grouped = work.tile([P, N_TILE, PACK], BF16, name="grouped", align_bytes=64)
             nc.vector.tensor_copy(
                 out=grouped[:, :width, :].rearrange("p (c i) t -> p c t i", i=RUN),
-                in_=xn[:, :, :width].rearrange("p t (c i) -> p c t i", i=RUN),
+                in_=xn[:, :, col : col + width].rearrange("p t (c i) -> p c t i", i=RUN),
             )
             return grouped
 
@@ -220,12 +221,20 @@ def tile_caps_bn_t_e_kernel(tc, x, weight_words, weight_scales, bias, out):
                 nc.sync.dma_start(out=out_view[n, o][:, col : col + width], in_=result[:, :width])
 
             units = [(first, width, g) for first, width in pixel_tiles() for g in range(PASSES)]
-            xn_next = normalise(*units[0])
+            xn_of_pass = [None] * PASSES
             accs = []
+
+            def prepare(first, width, g):
+                n, col = divmod(first, PIXELS)
+                if col == 0:
+                    xn_of_pass[g] = normalise(n, g)
+                return regroup(xn_of_pass[g], col, width)
+
+            grouped_next = prepare(*units[0])
             for u, (first, width, g) in enumerate(units):
-                grouped = regroup(xn_next, width)
+                grouped = grouped_next
                 if u + 1 < len(units):
-                    xn_next = normalise(*units[u + 1])
+                    grouped_next = prepare(*units[u + 1])
                 codes, plane = quantise(grouped, width)
                 if g == 0:
                     accs = [acc_banks.tile([P, N_TILE], F32, name="acc") for o in range(O_TILES)]

@@ -32,6 +32,7 @@ SUM_COLS = 128
 
 N_TILE = 512
 FIRST_TILE = 128
+FIRST_NORMALISED = 2 * FIRST_TILE
 O_TILES = CHANNELS // P
 RUN = 4
 
@@ -77,12 +78,16 @@ def tile_caps_bn_t_e_kernel(tc, x, weight_words, weight_scales, bias, out):
         bias_rows = const.tile([P, P], BF16, name="bias_rows")
         nc.vector.memset(bias_rows[:], 0.0)
 
+        nc.scalar.dma_start(out=bias_rows[0:O_TILES, :], in_=bias.rearrange("(o m) -> o m", m=P))
         x_sb = [[[None, None] for n in range(IMAGES)] for g in range(PASSES)]
         for g in range(PASSES):
             for n in range(IMAGES):
                 for a in (BY_VECTOR, BY_SCALAR):
                     x_sb[g][n][a] = x_pool.tile([P, HALF, PIXELS], BF16, name="x_%d_%d_%d" % (g, n, a))
-                    nc.sync.dma_start(out=x_sb[g][n][a][:], in_=x_view[n, g, a])
+                ends = (g, n) in ((0, 0), (PASSES - 1, IMAGES - 1))
+                for channels in ([slice(b, b + 1) for b in range(HALF)] if ends else [slice(0, HALF)]):
+                    for a in (BY_VECTOR, BY_SCALAR):
+                        nc.sync.dma_start(out=x_sb[g][n][a][:, channels, :], in_=x_view[n, g, a][:, channels, :])
         w_words = const.tile([P, PASSES, CHANNELS], U32, name="w_words", align_bytes=64)
         for g in range(PASSES):
             nc.sync.dma_start(
@@ -94,20 +99,32 @@ def tile_caps_bn_t_e_kernel(tc, x, weight_words, weight_scales, bias, out):
                 out=w_planes[32 * quadrant : 32 * quadrant + 4, :, :].bitcast(I32),
                 in_=weight_scales[:, 4 * quadrant : 4 * quadrant + 4, :].bitcast(I32).rearrange("g r n -> r g n"),
             )
-        nc.sync.dma_start(out=bias_rows[0:O_TILES, :], in_=bias.rearrange("(o m) -> o m", m=P))
 
-        mean_var = stat.tile([P, PASSES, PACK, 2], F32, name="mean_var")
-        rstd = stat.tile([P, PASSES, PACK], F32, name="rstd")
+        mean_var = [stat.tile([P, PASSES, HALF, 2], F32, name="mean_var_%d" % a) for a in (BY_VECTOR, BY_SCALAR)]
+        std = [stat.tile([P, PASSES, HALF], F32, name="std_%d" % a) for a in (BY_VECTOR, BY_SCALAR)]
+        rstd = [stat.tile([P, PASSES, HALF], F32, name="rstd_%d" % a) for a in (BY_VECTOR, BY_SCALAR)]
+        sums = stat.tile([P, PASSES, HALF], F32, name="sums")
         bias_col = const.tile([P, O_TILES], F32, name="bias_col")
-        scalar_ts = slice(BY_SCALAR * HALF, (BY_SCALAR + 1) * HALF)
 
         bn_out = stat.tile([P, PASSES, HALF, IMAGES * BN_PER_IMAGE, BN_WORDS], F32, name="bn_out")
         neg_shift = stat.tile([P, PASSES, HALF], F32, name="neg_shift")
         squares = stat.tile([P, PASSES, HALF, IMAGES], F32, name="squares")
         with tc.psum_pool(name="stat_banks", bufs=1) as stat_banks:
+            bias_ps = stat_banks.tile([P, P], BF16, name="bias_ps")
+            nc.tensor.transpose(bias_ps[:], bias_rows[:], ident[:])
+            nc.vector.tensor_copy(out=bias_col[:], in_=bias_ps[:, 0:O_TILES])
+
             sum_banks = [stat_banks.tile([P, HALF, SUM_COLS], F32, name="sum_bank_%d" % g) for g in range(PASSES)]
             for g in range(PASSES):
-                nc.scalar.mul(out=neg_shift[:, g, :], in_=x_sb[g][0][BY_SCALAR][:, :, 0], mul=-1.0)
+                for b in range(HALF):
+                    nc.gpsimd.tensor_scalar(
+                        out=neg_shift[:, g, b : b + 1],
+                        in0=x_sb[g][0][BY_SCALAR][:, b, 0:1],
+                        scalar1=-1.0,
+                        scalar2=0.0,
+                        op0=ALU.mult,
+                        op1=ALU.add,
+                    )
                 for n in range(IMAGES):
                     for b in range(HALF):
                         for c in range(BN_PER_IMAGE):
@@ -137,48 +154,44 @@ def tile_caps_bn_t_e_kernel(tc, x, weight_words, weight_scales, bias, out):
             for g in range(PASSES):
                 for b in range(HALF):
                     nc.vector.bn_aggr(
-                        out=mean_var[:, g, BY_VECTOR * HALF + b, :], in_=bn_out[:, g, b].rearrange("p c w -> p (c w)")
+                        out=mean_var[BY_VECTOR][:, g, b, :], in_=bn_out[:, g, b].rearrange("p c w -> p (c w)")
                     )
-            sums = stat.tile([P, PASSES, HALF], F32, name="sums")
-            for g in range(PASSES):
                 nc.vector.tensor_reduce(out=sums[:, g, :], in_=sum_banks[g][:], axis=AXIS.X, op=ALU.add)
-            nc.vector.tensor_scalar_mul(out=mean_var[:, :, scalar_ts, 0], in0=sums[:], scalar1=1.0 / SAMPLES)
+
+            def deviation(a):
+                nc.scalar.activation(out=std[a][:], in_=mean_var[a][:, :, :, 1], func=ACT.Sqrt, bias=EPS, scale=1.0)
+                nc.vector.reciprocal(out=rstd[a][:], in_=std[a][:])
+
+            deviation(BY_VECTOR)
+            nc.vector.tensor_scalar_mul(out=mean_var[BY_SCALAR][:, :, :, 0], in0=sums[:], scalar1=1.0 / SAMPLES)
             offset = stat.tile([P, PASSES, HALF], F32, name="offset")
             nc.vector.scalar_tensor_tensor(
                 out=offset[:], in0=sums[:], scalar=1.0 / SAMPLES, in1=neg_shift[:], op0=ALU.mult, op1=ALU.add
             )
-            offset_sq = stat.tile([P, PASSES, HALF], F32, name="offset_sq")
-            nc.vector.tensor_mul(out=offset_sq[:], in0=offset[:], in1=offset[:])
             square_sums = stat.tile([P, PASSES, HALF], F32, name="square_sums")
             nc.vector.tensor_reduce(out=square_sums[:], in_=squares[:], axis=AXIS.X, op=ALU.add)
+            offset_sq = stat.tile([P, PASSES, HALF], F32, name="offset_sq")
+            nc.vector.tensor_mul(out=offset_sq[:], in0=offset[:], in1=offset[:])
             nc.vector.scalar_tensor_tensor(
-                out=mean_var[:, :, scalar_ts, 1],
+                out=mean_var[BY_SCALAR][:, :, :, 1],
                 in0=square_sums[:],
                 scalar=1.0 / SAMPLES,
                 in1=offset_sq[:],
                 op0=ALU.mult,
                 op1=ALU.subtract,
             )
-            std = stat.tile([P, PASSES, PACK], F32, name="std")
-            nc.scalar.activation(out=std[:], in_=mean_var[:, :, :, 1], func=ACT.Sqrt, bias=EPS, scale=1.0)
-            nc.vector.reciprocal(out=rstd[:], in_=std[:])
+            deviation(BY_SCALAR)
 
-            bias_ps = stat_banks.tile([P, P], BF16, name="bias_ps")
-            nc.tensor.transpose(bias_ps[:], bias_rows[:], ident[:])
-            nc.vector.tensor_copy(out=bias_col[:], in_=bias_ps[:, 0:O_TILES])
-
-        def normalise(n, g):
-            xn = images.tile([P, PACK, PIXELS], BF16, name="xn")
-            for t in range(PACK):
+        def normalise(xn, n, g, a, cols):
+            for b in range(HALF):
                 nc.vector.tensor_scalar(
-                    out=xn[:, t, :],
-                    in0=x_sb[g][n][t // HALF][:, t % HALF, :],
-                    scalar1=mean_var[:, g, t, 0:1],
-                    scalar2=rstd[:, g, t : t + 1],
+                    out=xn[:, a * HALF + b, cols],
+                    in0=x_sb[g][n][a][:, b, cols],
+                    scalar1=mean_var[a][:, g, b, 0:1],
+                    scalar2=rstd[a][:, g, b : b + 1],
                     op0=ALU.subtract,
                     op1=ALU.mult,
                 )
-            return xn
 
         def regroup(xn, col, width):
             grouped = work.tile([P, N_TILE, PACK], BF16, name="grouped", align_bytes=64)
@@ -222,12 +235,22 @@ def tile_caps_bn_t_e_kernel(tc, x, weight_words, weight_scales, bias, out):
 
             units = [(first, width, g) for first, width in pixel_tiles() for g in range(PASSES)]
             xn_of_pass = [None] * PASSES
-            accs = []
+            operands = [None] * PASSES
 
             def prepare(first, width, g):
                 n, col = divmod(first, PIXELS)
-                if col == 0:
-                    xn_of_pass[g] = normalise(n, g)
+                if first == 0:
+                    if g == 0:
+                        for h in range(PASSES):
+                            xn_of_pass[h] = images.tile([P, PACK, PIXELS], BF16, name="xn")
+                        for a in (BY_VECTOR, BY_SCALAR):
+                            for h in range(PASSES):
+                                normalise(xn_of_pass[h], n, h, a, slice(0, FIRST_NORMALISED))
+                elif first == FIRST_NORMALISED or col == 0:
+                    if col == 0:
+                        xn_of_pass[g] = images.tile([P, PACK, PIXELS], BF16, name="xn")
+                    for a in (BY_VECTOR, BY_SCALAR):
+                        normalise(xn_of_pass[g], n, g, a, slice(col, PIXELS))
                 return regroup(xn_of_pass[g], col, width)
 
             grouped_next = prepare(*units[0])
@@ -235,10 +258,10 @@ def tile_caps_bn_t_e_kernel(tc, x, weight_words, weight_scales, bias, out):
                 grouped = grouped_next
                 if u + 1 < len(units):
                     grouped_next = prepare(*units[u + 1])
-                codes, plane = quantise(grouped, width)
-                if g == 0:
-                    accs = [acc_banks.tile([P, N_TILE], F32, name="acc") for o in range(O_TILES)]
-                for o in range(O_TILES):
-                    multiply(accs[o], o, g, codes, plane, width)
-                    if g == PASSES - 1:
-                        add_bias_and_store(accs[o], o, first, width)
+                operands[g] = quantise(grouped, width)
+                if g == PASSES - 1:
+                    for o in range(O_TILES):
+                        acc = acc_banks.tile([P, N_TILE], F32, name="acc")
+                        for h, (codes, plane) in enumerate(operands):
+                            multiply(acc, o, h, codes, plane, width)
+                        add_bias_and_store(acc, o, first, width)

@@ -34,6 +34,7 @@ N_TILE = 512
 FIRST_TILE = 128
 FIRST_NORMALISED = 2 * FIRST_TILE
 O_TILES = CHANNELS // P
+O_STORE = 2
 RUN = 4
 
 FLOPS = 2 * CHANNELS * CHANNELS * IMAGES * PIXELS
@@ -53,7 +54,7 @@ def pixel_tiles():
 def tile_caps_bn_t_e_kernel(tc, x, weight_words, weight_scales, bias, out):
     nc = tc.nc
     x_view = x.rearrange("n (g p a b) h w -> n g a p b (h w)", g=PASSES, p=P, a=PACK // HALF, b=HALF)
-    out_view = out.rearrange("n (o m) h w -> n o m (h w)", m=P)
+    out_view = out.rearrange("n (o m) h w -> n m o (h w)", m=P)
 
     with ExitStack() as pools:
         const = pools.enter_context(tc.tile_pool(name="const", bufs=1))
@@ -63,7 +64,7 @@ def tile_caps_bn_t_e_kernel(tc, x, weight_words, weight_scales, bias, out):
         images = pools.enter_context(tc.tile_pool(name="images", bufs=4))
         work = pools.enter_context(tc.tile_pool(name="work", bufs=4))
         quant = pools.enter_context(tc.tile_pool(name="quant", bufs=8))
-        results = pools.enter_context(tc.tile_pool(name="results", bufs=12))
+        results = pools.enter_context(tc.tile_pool(name="results", bufs=8))
 
         one_col = const.tile([P, 1], F32, name="one_col")
         nc.vector.memset(one_col[:], 1.0)
@@ -225,13 +226,20 @@ def tile_caps_bn_t_e_kernel(tc, x, weight_words, weight_scales, bias, out):
                     stop=(g == PASSES - 1),
                 )
 
-            def add_bias_and_store(acc, o, first, width):
-                n, col = divmod(first, PIXELS)
-                result = results.tile([P, N_TILE], F32, name="result")
+            def add_bias(result, acc, o, width):
                 nc.scalar.activation(
-                    out=result[:, :width], in_=acc[:, :width], func=ACT.Identity, bias=bias_col[:, o : o + 1], scale=1.0
+                    out=result[:, o % O_STORE, :width],
+                    in_=acc[:, :width],
+                    func=ACT.Identity,
+                    bias=bias_col[:, o : o + 1],
+                    scale=1.0,
                 )
-                nc.sync.dma_start(out=out_view[n, o][:, col : col + width], in_=result[:, :width])
+
+            def store(result, o, first, width):
+                n, col = divmod(first, PIXELS)
+                nc.sync.dma_start(
+                    out=out_view[n, :, o - O_STORE + 1 : o + 1, col : col + width], in_=result[:, :, :width]
+                )
 
             units = [(first, width, g) for first, width in pixel_tiles() for g in range(PASSES)]
             xn_of_pass = [None] * PASSES
@@ -264,4 +272,8 @@ def tile_caps_bn_t_e_kernel(tc, x, weight_words, weight_scales, bias, out):
                         acc = acc_banks.tile([P, N_TILE], F32, name="acc")
                         for h, (codes, plane) in enumerate(operands):
                             multiply(acc, o, h, codes, plane, width)
-                        add_bias_and_store(acc, o, first, width)
+                        if o % O_STORE == 0:
+                            result = results.tile([P, O_STORE, N_TILE], F32, name="result")
+                        add_bias(result, acc, o, width)
+                        if o % O_STORE == O_STORE - 1:
+                            store(result, o, first, width)

@@ -51,6 +51,10 @@ def pixel_tiles():
     return tiles
 
 
+def vector_banks(first, width):
+    return range(1, O_TILES, 2) if first + width == IMAGES * PIXELS else ()
+
+
 def tile_caps_bn_t_e_kernel(tc, x, weight_words, weight_scales, bias, out):
     nc = tc.nc
     x_view = x.rearrange("n (g p a b) h w -> n g a p b (h w)", g=PASSES, p=P, a=PACK // HALF, b=HALF)
@@ -79,16 +83,15 @@ def tile_caps_bn_t_e_kernel(tc, x, weight_words, weight_scales, bias, out):
         bias_rows = const.tile([P, P], BF16, name="bias_rows")
         nc.vector.memset(bias_rows[:], 0.0)
 
-        nc.scalar.dma_start(out=bias_rows[0:O_TILES, :], in_=bias.rearrange("(o m) -> o m", m=P))
         x_sb = [[[None, None] for n in range(IMAGES)] for g in range(PASSES)]
         for g in range(PASSES):
             for n in range(IMAGES):
                 for a in (BY_VECTOR, BY_SCALAR):
                     x_sb[g][n][a] = x_pool.tile([P, HALF, PIXELS], BF16, name="x_%d_%d_%d" % (g, n, a))
-                ends = (g, n) in ((0, 0), (PASSES - 1, IMAGES - 1))
-                for channels in ([slice(b, b + 1) for b in range(HALF)] if ends else [slice(0, HALF)]):
-                    for a in (BY_VECTOR, BY_SCALAR):
-                        nc.sync.dma_start(out=x_sb[g][n][a][:, channels, :], in_=x_view[n, g, a][:, channels, :])
+                for a in (BY_VECTOR, BY_SCALAR):
+                    nc.sync.dma_start(out=x_sb[g][n][a][:], in_=x_view[n, g, a])
+                if (g, n) == (0, 0):
+                    nc.sync.dma_start(out=bias_rows[0:O_TILES, :], in_=bias.rearrange("(o m) -> o m", m=P))
         w_words = const.tile([P, PASSES, CHANNELS], U32, name="w_words", align_bytes=64)
         for g in range(PASSES):
             nc.sync.dma_start(
@@ -111,21 +114,9 @@ def tile_caps_bn_t_e_kernel(tc, x, weight_words, weight_scales, bias, out):
         neg_shift = stat.tile([P, PASSES, HALF], F32, name="neg_shift")
         squares = stat.tile([P, PASSES, HALF, IMAGES], F32, name="squares")
         with tc.psum_pool(name="stat_banks", bufs=1) as stat_banks:
-            bias_ps = stat_banks.tile([P, P], BF16, name="bias_ps")
-            nc.tensor.transpose(bias_ps[:], bias_rows[:], ident[:])
-            nc.vector.tensor_copy(out=bias_col[:], in_=bias_ps[:, 0:O_TILES])
-
             sum_banks = [stat_banks.tile([P, HALF, SUM_COLS], F32, name="sum_bank_%d" % g) for g in range(PASSES)]
             for g in range(PASSES):
-                for b in range(HALF):
-                    nc.gpsimd.tensor_scalar(
-                        out=neg_shift[:, g, b : b + 1],
-                        in0=x_sb[g][0][BY_SCALAR][:, b, 0:1],
-                        scalar1=-1.0,
-                        scalar2=0.0,
-                        op0=ALU.mult,
-                        op1=ALU.add,
-                    )
+                nc.scalar.mul(out=neg_shift[:, g, :], in_=x_sb[g][0][BY_SCALAR][:, :, 0], mul=-1.0)
                 for n in range(IMAGES):
                     for b in range(HALF):
                         for c in range(BN_PER_IMAGE):
@@ -151,6 +142,10 @@ def tile_caps_bn_t_e_kernel(tc, x, weight_words, weight_scales, bias, out):
                             start=(n == 0 and c == 0),
                             stop=(n == IMAGES - 1 and c == PIXELS // SUM_COLS - 1),
                         )
+
+            bias_ps = stat_banks.tile([P, P], BF16, name="bias_ps")
+            nc.tensor.transpose(bias_ps[:], bias_rows[:], ident[:])
+            nc.vector.tensor_copy(out=bias_col[:], in_=bias_ps[:, 0:O_TILES])
 
             for g in range(PASSES):
                 for b in range(HALF):
@@ -226,14 +221,16 @@ def tile_caps_bn_t_e_kernel(tc, x, weight_words, weight_scales, bias, out):
                     stop=(g == PASSES - 1),
                 )
 
-            def add_bias(result, acc, o, width):
-                nc.scalar.activation(
-                    out=result[:, o % O_STORE, :width],
-                    in_=acc[:, :width],
-                    func=ACT.Identity,
-                    bias=bias_col[:, o : o + 1],
-                    scale=1.0,
-                )
+            def add_bias(result, acc, o, first, width):
+                part = result[:, o % O_STORE, :width]
+                if o in vector_banks(first, width):
+                    nc.vector.tensor_scalar(
+                        out=part, in0=acc[:, :width], scalar1=bias_col[:, o : o + 1], scalar2=None, op0=ALU.add
+                    )
+                else:
+                    nc.scalar.activation(
+                        out=part, in_=acc[:, :width], func=ACT.Identity, bias=bias_col[:, o : o + 1], scale=1.0
+                    )
 
             def store(result, o, first, width):
                 n, col = divmod(first, PIXELS)
@@ -274,6 +271,6 @@ def tile_caps_bn_t_e_kernel(tc, x, weight_words, weight_scales, bias, out):
                             multiply(acc, o, h, codes, plane, width)
                         if o % O_STORE == 0:
                             result = results.tile([P, O_STORE, N_TILE], F32, name="result")
-                        add_bias(result, acc, o, width)
+                        add_bias(result, acc, o, first, width)
                         if o % O_STORE == O_STORE - 1:
                             store(result, o, first, width)

@@ -78,7 +78,7 @@ def tile_caps_bn_t_e_kernel(tc, x, weight_words, weight_scales, bias, out):
         ident = const.tile([P, P], BF16, name="ident")
         make_identity(nc, ident[:])
 
-        w_planes = const.tile([P, PASSES, CHANNELS], U8, name="w_planes", align_bytes=64)
+        w_planes = const.tile([P, PASSES, CHANNELS], U8, name="w_planes", align_bytes=256)
         nc.vector.memset(w_planes[:].bitcast(I32), 0)
         bias_rows = const.tile([P, P], BF16, name="bias_rows")
         nc.vector.memset(bias_rows[:], 0.0)
@@ -92,7 +92,7 @@ def tile_caps_bn_t_e_kernel(tc, x, weight_words, weight_scales, bias, out):
                     nc.sync.dma_start(out=x_sb[g][n][a][:], in_=x_view[n, g, a])
                 if (g, n) == (0, 0):
                     nc.sync.dma_start(out=bias_rows[0:O_TILES, :], in_=bias.rearrange("(o m) -> o m", m=P))
-        w_words = const.tile([P, PASSES, CHANNELS], U32, name="w_words", align_bytes=64)
+        w_words = const.tile([P, PASSES, CHANNELS], U32, name="w_words", align_bytes=256)
         for g in range(PASSES):
             nc.sync.dma_start(
                 out=w_words[:, g, :].bitcast(I32),
@@ -190,7 +190,7 @@ def tile_caps_bn_t_e_kernel(tc, x, weight_words, weight_scales, bias, out):
                 )
 
         def regroup(xn, col, width):
-            grouped = work.tile([P, N_TILE, PACK], BF16, name="grouped", align_bytes=64)
+            grouped = work.tile([P, N_TILE, PACK], BF16, name="grouped", align_bytes=256)
             nc.vector.tensor_copy(
                 out=grouped[:, :width, :].rearrange("p (c i) t -> p c t i", i=RUN),
                 in_=xn[:, :, col : col + width].rearrange("p t (c i) -> p c t i", i=RUN),
@@ -198,8 +198,8 @@ def tile_caps_bn_t_e_kernel(tc, x, weight_words, weight_scales, bias, out):
             return grouped
 
         def quantise(grouped, width):
-            codes = quant.tile([P, N_TILE], U32, name="codes", align_bytes=64)
-            plane = quant.tile([P, N_TILE], U8, name="plane", align_bytes=64)
+            codes = quant.tile([P, N_TILE], U32, name="codes", align_bytes=256)
+            plane = quant.tile([P, N_TILE], U8, name="plane", align_bytes=256)
             nc.vector.quantize_mx(
                 out=codes[:, :width].bitcast(FP8X4),
                 scales=plane[:, :width],

@@ -28,6 +28,7 @@ BY_SCALAR = 1
 BN_CHUNK = 512
 BN_PER_IMAGE = PIXELS // BN_CHUNK
 BN_WORDS = 6
+CLOSE_IMAGE = 1
 SUM_COLS = 128
 
 N_TILE = 512
@@ -73,7 +74,7 @@ def tile_caps_bn_t_e_kernel(tc, x, weight_words, weight_scales, bias, out):
         one_col = const.tile([P, 1], F32, name="one_col")
         nc.vector.memset(one_col[:], 1.0)
         table_warm = const.tile([P, 1], F32, name="table_warm")
-        nc.scalar.activation(out=table_warm[:], in_=one_col[:], func=ACT.Sqrt)
+        nc.scalar.activation(out=table_warm[:], in_=one_col[:], func=ACT.Abs_reciprocal_sqrt)
 
         ident = const.tile([P, P], BF16, name="ident")
         make_identity(nc, ident[:])
@@ -105,7 +106,6 @@ def tile_caps_bn_t_e_kernel(tc, x, weight_words, weight_scales, bias, out):
             )
 
         mean_var = [stat.tile([P, PASSES, HALF, 2], F32, name="mean_var_%d" % a) for a in (BY_VECTOR, BY_SCALAR)]
-        std = [stat.tile([P, PASSES, HALF], F32, name="std_%d" % a) for a in (BY_VECTOR, BY_SCALAR)]
         rstd = [stat.tile([P, PASSES, HALF], F32, name="rstd_%d" % a) for a in (BY_VECTOR, BY_SCALAR)]
         sums = stat.tile([P, PASSES, HALF], F32, name="sums")
         bias_col = const.tile([P, O_TILES], F32, name="bias_col")
@@ -115,6 +115,14 @@ def tile_caps_bn_t_e_kernel(tc, x, weight_words, weight_scales, bias, out):
         squares = stat.tile([P, PASSES, HALF, IMAGES], F32, name="squares")
         with tc.psum_pool(name="stat_banks", bufs=1) as stat_banks:
             sum_banks = [stat_banks.tile([P, HALF, SUM_COLS], F32, name="sum_bank_%d" % g) for g in range(PASSES)]
+
+            def close_pass(g):
+                for b in range(HALF):
+                    nc.vector.bn_aggr(
+                        out=mean_var[BY_VECTOR][:, g, b, :], in_=bn_out[:, g, b].rearrange("p c w -> p (c w)")
+                    )
+                nc.vector.tensor_reduce(out=sums[:, g, :], in_=sum_banks[g][:], axis=AXIS.X, op=ALU.add)
+
             for g in range(PASSES):
                 nc.scalar.mul(out=neg_shift[:, g, :], in_=x_sb[g][0][BY_SCALAR][:, :, 0], mul=-1.0)
                 for n in range(IMAGES):
@@ -142,21 +150,19 @@ def tile_caps_bn_t_e_kernel(tc, x, weight_words, weight_scales, bias, out):
                             start=(n == 0 and c == 0),
                             stop=(n == IMAGES - 1 and c == PIXELS // SUM_COLS - 1),
                         )
+                    if g > 0 and n == CLOSE_IMAGE:
+                        close_pass(g - 1)
 
             bias_ps = stat_banks.tile([P, P], BF16, name="bias_ps")
             nc.tensor.transpose(bias_ps[:], bias_rows[:], ident[:])
             nc.vector.tensor_copy(out=bias_col[:], in_=bias_ps[:, 0:O_TILES])
 
-            for g in range(PASSES):
-                for b in range(HALF):
-                    nc.vector.bn_aggr(
-                        out=mean_var[BY_VECTOR][:, g, b, :], in_=bn_out[:, g, b].rearrange("p c w -> p (c w)")
-                    )
-                nc.vector.tensor_reduce(out=sums[:, g, :], in_=sum_banks[g][:], axis=AXIS.X, op=ALU.add)
+            close_pass(PASSES - 1)
 
             def deviation(a):
-                nc.scalar.activation(out=std[a][:], in_=mean_var[a][:, :, :, 1], func=ACT.Sqrt, bias=EPS, scale=1.0)
-                nc.vector.reciprocal(out=rstd[a][:], in_=std[a][:])
+                nc.scalar.activation(
+                    out=rstd[a][:], in_=mean_var[a][:, :, :, 1], func=ACT.Abs_reciprocal_sqrt, bias=EPS, scale=1.0
+                )
 
             deviation(BY_VECTOR)
             nc.vector.tensor_scalar_mul(out=mean_var[BY_SCALAR][:, :, :, 0], in0=sums[:], scalar1=1.0 / SAMPLES)

@@ -105,7 +105,11 @@ def tile_caps_bn_t_e_kernel(tc, x, weight_words, weight_scales, bias, out):
                 in_=weight_scales[:, 4 * quadrant : 4 * quadrant + 4, :].bitcast(I32).rearrange("g r n -> r g n"),
             )
 
-        mean_var = [stat.tile([P, PASSES, HALF, 2], F32, name="mean_var_%d" % a) for a in (BY_VECTOR, BY_SCALAR)]
+        mean_var_v = stat.tile([P, PASSES, HALF, 2], F32, name="mean_var_v")
+        mean_s = stat.tile([P, PASSES, HALF], F32, name="mean_s")
+        var_s = stat.tile([P, PASSES, HALF], F32, name="var_s")
+        mean = [mean_var_v[:, :, :, 0], mean_s[:]]
+        var = [mean_var_v[:, :, :, 1], var_s[:]]
         rstd = [stat.tile([P, PASSES, HALF], F32, name="rstd_%d" % a) for a in (BY_VECTOR, BY_SCALAR)]
         sums = stat.tile([P, PASSES, HALF], F32, name="sums")
         bias_col = const.tile([P, O_TILES], F32, name="bias_col")
@@ -119,7 +123,7 @@ def tile_caps_bn_t_e_kernel(tc, x, weight_words, weight_scales, bias, out):
             def close_pass(g):
                 for b in range(HALF):
                     nc.vector.bn_aggr(
-                        out=mean_var[BY_VECTOR][:, g, b, :], in_=bn_out[:, g, b].rearrange("p c w -> p (c w)")
+                        out=mean_var_v[:, g, b, :], in_=bn_out[:, g, b].rearrange("p c w -> p (c w)")
                     )
                 nc.vector.tensor_reduce(out=sums[:, g, :], in_=sum_banks[g][:], axis=AXIS.X, op=ALU.add)
 
@@ -161,26 +165,37 @@ def tile_caps_bn_t_e_kernel(tc, x, weight_words, weight_scales, bias, out):
 
             def deviation(a):
                 nc.scalar.activation(
-                    out=rstd[a][:], in_=mean_var[a][:, :, :, 1], func=ACT.Abs_reciprocal_sqrt, bias=EPS, scale=1.0
+                    out=rstd[a][:], in_=var[a], func=ACT.Abs_reciprocal_sqrt, bias=EPS, scale=1.0
                 )
 
             deviation(BY_VECTOR)
-            nc.vector.tensor_scalar_mul(out=mean_var[BY_SCALAR][:, :, :, 0], in0=sums[:], scalar1=1.0 / SAMPLES)
-            offset = stat.tile([P, PASSES, HALF], F32, name="offset")
-            nc.vector.scalar_tensor_tensor(
-                out=offset[:], in0=sums[:], scalar=1.0 / SAMPLES, in1=neg_shift[:], op0=ALU.mult, op1=ALU.add
+            def small(name):
+                return stat.tile([P, PASSES, HALF], F32, name=name)
+
+            early_squares = small("early_squares")
+            nc.gpsimd.tensor_add(out=early_squares[:], in0=squares[:, :, :, 0], in1=squares[:, :, :, 1])
+            for n in range(2, IMAGES - 1):
+                nc.gpsimd.tensor_add(out=early_squares[:], in0=early_squares[:], in1=squares[:, :, :, n])
+            early_mean_sq = small("early_mean_sq")
+            nc.gpsimd.tensor_scalar(
+                out=early_mean_sq[:], in0=early_squares[:], scalar1=1.0 / SAMPLES, scalar2=0.0, op0=ALU.mult, op1=ALU.add
             )
-            square_sums = stat.tile([P, PASSES, HALF], F32, name="square_sums")
-            nc.vector.tensor_reduce(out=square_sums[:], in_=squares[:], axis=AXIS.X, op=ALU.add)
-            offset_sq = stat.tile([P, PASSES, HALF], F32, name="offset_sq")
-            nc.vector.tensor_mul(out=offset_sq[:], in0=offset[:], in1=offset[:])
+            nc.gpsimd.tensor_scalar(
+                out=mean[BY_SCALAR], in0=sums[:], scalar1=1.0 / SAMPLES, scalar2=0.0, op0=ALU.mult, op1=ALU.add
+            )
+            offset = small("offset")
+            nc.gpsimd.tensor_add(out=offset[:], in0=mean[BY_SCALAR], in1=neg_shift[:])
+            offset_sq = small("offset_sq")
+            nc.gpsimd.tensor_mul(out=offset_sq[:], in0=offset[:], in1=offset[:])
+            var_rest = small("var_rest")
+            nc.gpsimd.tensor_sub(out=var_rest[:], in0=early_mean_sq[:], in1=offset_sq[:])
             nc.vector.scalar_tensor_tensor(
-                out=mean_var[BY_SCALAR][:, :, :, 1],
-                in0=square_sums[:],
+                out=var[BY_SCALAR],
+                in0=squares[:, :, :, IMAGES - 1],
                 scalar=1.0 / SAMPLES,
-                in1=offset_sq[:],
+                in1=var_rest[:],
                 op0=ALU.mult,
-                op1=ALU.subtract,
+                op1=ALU.add,
             )
             deviation(BY_SCALAR)
 
@@ -189,15 +204,15 @@ def tile_caps_bn_t_e_kernel(tc, x, weight_words, weight_scales, bias, out):
                 nc.vector.tensor_scalar(
                     out=xn[:, a * HALF + b, cols],
                     in0=x_sb[g][n][a][:, b, cols],
-                    scalar1=mean_var[a][:, g, b, 0:1],
+                    scalar1=mean[a][:, g, b : b + 1],
                     scalar2=rstd[a][:, g, b : b + 1],
                     op0=ALU.subtract,
                     op1=ALU.mult,
                 )
 
-        def regroup(xn, col, width):
+        def regroup(xn, col, width, copy):
             grouped = work.tile([P, N_TILE, PACK], BF16, name="grouped", align_bytes=256)
-            nc.vector.tensor_copy(
+            copy(
                 out=grouped[:, :width, :].rearrange("p (c i) t -> p c t i", i=RUN),
                 in_=xn[:, :, col : col + width].rearrange("p t (c i) -> p c t i", i=RUN),
             )
@@ -262,7 +277,8 @@ def tile_caps_bn_t_e_kernel(tc, x, weight_words, weight_scales, bias, out):
                         xn_of_pass[g] = images.tile([P, PACK, PIXELS], BF16, name="xn")
                     for a in (BY_VECTOR, BY_SCALAR):
                         normalise(xn_of_pass[g], n, g, a, slice(col, PIXELS))
-                return regroup(xn_of_pass[g], col, width)
+                by_scalar = g == 0 and first < FIRST_NORMALISED
+                return regroup(xn_of_pass[g], col, width, nc.scalar.copy if by_scalar else nc.vector.tensor_copy)
 
             grouped_next = prepare(*units[0])
             for u, (first, width, g) in enumerate(units):

@@ -89,8 +89,13 @@ def tile_caps_bn_t_e_kernel(tc, x, weight_words, weight_scales, bias, out):
             for n in range(IMAGES):
                 for a in (BY_VECTOR, BY_SCALAR):
                     x_sb[g][n][a] = x_pool.tile([P, HALF, PIXELS], BF16, name="x_%d_%d_%d" % (g, n, a))
-                for a in (BY_VECTOR, BY_SCALAR):
-                    nc.sync.dma_start(out=x_sb[g][n][a][:], in_=x_view[n, g, a])
+                if (g, n) == (PASSES - 1, IMAGES - 1):
+                    for b in range(HALF):
+                        for a in (BY_VECTOR, BY_SCALAR):
+                            nc.sync.dma_start(out=x_sb[g][n][a][:, b, :], in_=x_view[n, g, a, :, b, :])
+                else:
+                    for a in (BY_VECTOR, BY_SCALAR):
+                        nc.sync.dma_start(out=x_sb[g][n][a][:], in_=x_view[n, g, a])
                 if (g, n) == (0, 0):
                     nc.sync.dma_start(out=bias_rows[0:O_TILES, :], in_=bias.rearrange("(o m) -> o m", m=P))
         w_words = const.tile([P, PASSES, CHANNELS], U32, name="w_words", align_bytes=256)

@@ -282,7 +282,7 @@ def tile_caps_bn_t_e_kernel(tc, x, weight_words, weight_scales, bias, out):
                         xn_of_pass[g] = images.tile([P, PACK, PIXELS], BF16, name="xn")
                     for a in (BY_VECTOR, BY_SCALAR):
                         normalise(xn_of_pass[g], n, g, a, slice(col, PIXELS))
-                by_scalar = g == 0 and first < FIRST_NORMALISED
+                by_scalar = g == 0 and width < N_TILE
                 return regroup(xn_of_pass[g], col, width, nc.scalar.copy if by_scalar else nc.vector.tensor_copy)
 
             grouped_next = prepare(*units[0])

from contextlib import ExitStack

import concourse.mybir as mybir
from concourse.masks import make_identity

F32 = mybir.dt.float32
BF16 = mybir.dt.bfloat16
I32 = mybir.dt.int32
U32 = mybir.dt.uint32
U8 = mybir.dt.uint8
FP8X4 = mybir.dt.float8_e4m3fn_x4
ALU = mybir.AluOpType
ACT = mybir.ActivationFunctionType
AXIS = mybir.AxisListType

P = 128
PACK = 4
IMAGES = 4
CHANNELS = 1024
PIXELS = 1024
PASSES = CHANNELS // (P * PACK)
SAMPLES = IMAGES * PIXELS
EPS = 1e-5

HALF = PACK // 2
BY_VECTOR = 0
BY_SCALAR = 1
BN_CHUNK = 512
BN_PER_IMAGE = PIXELS // BN_CHUNK
BN_WORDS = 6
CLOSE_IMAGE = 1
SUM_COLS = 128

N_TILE = 512
FIRST_TILE = 128
FIRST_NORMALISED = 2 * FIRST_TILE
O_TILES = CHANNELS // P
O_STORE = 2
RUN = 4

FLOPS = 2 * CHANNELS * CHANNELS * IMAGES * PIXELS


def pixel_tiles():
    tiles = []
    first = 0
    width = FIRST_TILE
    while first < IMAGES * PIXELS:
        tiles.append((first, width))
        first += width
        width = min(first, N_TILE)
    return tiles


def vector_banks(first, width):
    return range(1, O_TILES, 2) if first + width == IMAGES * PIXELS else ()


def tile_caps_bn_t_e_kernel(tc, x, weight_words, weight_scales, bias, out):
    nc = tc.nc
    x_view = x.rearrange("n (g p a b) h w -> n g a p b (h w)", g=PASSES, p=P, a=PACK // HALF, b=HALF)
    out_view = out.rearrange("n (o m) h w -> n m o (h w)", m=P)

    with ExitStack() as pools:
        const = pools.enter_context(tc.tile_pool(name="const", bufs=1))
        x_pool = pools.enter_context(tc.tile_pool(name="x_pool", bufs=1))
        stat = pools.enter_context(tc.tile_pool(name="stat", bufs=1))
        scratch = pools.enter_context(tc.tile_pool(name="scratch", bufs=4))
        images = pools.enter_context(tc.tile_pool(name="images", bufs=4))
        work = pools.enter_context(tc.tile_pool(name="work", bufs=4))
        quant = pools.enter_context(tc.tile_pool(name="quant", bufs=8))
        results = pools.enter_context(tc.tile_pool(name="results", bufs=8))

        one_col = const.tile([P, 1], F32, name="one_col")
        nc.vector.memset(one_col[:], 1.0)
        table_warm = const.tile([P, 1], F32, name="table_warm")
        nc.scalar.activation(out=table_warm[:], in_=one_col[:], func=ACT.Abs_reciprocal_sqrt)

        ident = const.tile([P, P], BF16, name="ident")
        make_identity(nc, ident[:])

        w_planes = const.tile([P, PASSES, CHANNELS], U8, name="w_planes", align_bytes=256)
        nc.vector.memset(w_planes[:].bitcast(I32), 0)
        bias_rows = const.tile([P, P], BF16, name="bias_rows")
        nc.vector.memset(bias_rows[:], 0.0)

        x_sb = [[[None, None] for n in range(IMAGES)] for g in range(PASSES)]
        for g in range(PASSES):
            for n in range(IMAGES):
                for a in (BY_VECTOR, BY_SCALAR):
                    x_sb[g][n][a] = x_pool.tile([P, HALF, PIXELS], BF16, name="x_%d_%d_%d" % (g, n, a))
                if (g, n) == (PASSES - 1, IMAGES - 1):
                    for b in range(HALF):
                        for a in (BY_VECTOR, BY_SCALAR):
                            nc.sync.dma_start(out=x_sb[g][n][a][:, b, :], in_=x_view[n, g, a, :, b, :])
                else:
                    for a in (BY_VECTOR, BY_SCALAR):
                        nc.sync.dma_start(out=x_sb[g][n][a][:], in_=x_view[n, g, a])
                if (g, n) == (0, 0):
                    nc.sync.dma_start(out=bias_rows[0:O_TILES, :], in_=bias.rearrange("(o m) -> o m", m=P))
        w_words = const.tile([P, PASSES, CHANNELS], U32, name="w_words", align_bytes=256)
        for g in range(PASSES):
            nc.sync.dma_start(
                out=w_words[:, g, :].bitcast(I32),
                in_=weight_words[g].rearrange("p n t -> p (n t)").bitcast(I32),
            )
        for quadrant in range(4):
            nc.sync.dma_start(
                out=w_planes[32 * quadrant : 32 * quadrant + 4, :, :].bitcast(I32),
                in_=weight_scales[:, 4 * quadrant : 4 * quadrant + 4, :].bitcast(I32).rearrange("g r n -> r g n"),
            )

        mean_var_v = stat.tile([P, PASSES, HALF, 2], F32, name="mean_var_v")
        mean_s = stat.tile([P, PASSES, HALF], F32, name="mean_s")
        var_s = stat.tile([P, PASSES, HALF], F32, name="var_s")
        mean = [mean_var_v[:, :, :, 0], mean_s[:]]
        var = [mean_var_v[:, :, :, 1], var_s[:]]
        rstd = [stat.tile([P, PASSES, HALF], F32, name="rstd_%d" % a) for a in (BY_VECTOR, BY_SCALAR)]
        sums = stat.tile([P, PASSES, HALF], F32, name="sums")
        bias_col = const.tile([P, O_TILES], F32, name="bias_col")

        bn_out = stat.tile([P, PASSES, HALF, IMAGES * BN_PER_IMAGE, BN_WORDS], F32, name="bn_out")
        neg_shift = stat.tile([P, PASSES, HALF], F32, name="neg_shift")
        squares = stat.tile([P, PASSES, HALF, IMAGES], F32, name="squares")
        with tc.psum_pool(name="stat_banks", bufs=1) as stat_banks:
            sum_banks = [stat_banks.tile([P, HALF, SUM_COLS], F32, name="sum_bank_%d" % g) for g in range(PASSES)]

            def close_pass(g):
                for b in range(HALF):
                    nc.vector.bn_aggr(
                        out=mean_var_v[:, g, b, :], in_=bn_out[:, g, b].rearrange("p c w -> p (c w)")
                    )
                nc.vector.tensor_reduce(out=sums[:, g, :], in_=sum_banks[g][:], axis=AXIS.X, op=ALU.add)

            for g in range(PASSES):
                nc.scalar.mul(out=neg_shift[:, g, :], in_=x_sb[g][0][BY_SCALAR][:, :, 0], mul=-1.0)
                for n in range(IMAGES):
                    for b in range(HALF):
                        for c in range(BN_PER_IMAGE):
                            nc.vector.bn_stats(
                                out=bn_out[:, g, b, n * BN_PER_IMAGE + c, :],
                                in_=x_sb[g][n][BY_VECTOR][:, b, c * BN_CHUNK : (c + 1) * BN_CHUNK],
                            )
                    for b in range(HALF):
                        unread = scratch.tile([P, PIXELS], BF16, name="unread")
                        nc.scalar.activation(
                            out=unread[:],
                            in_=x_sb[g][n][BY_SCALAR][:, b, :],
                            func=ACT.Square,
                            bias=neg_shift[:, g, b : b + 1],
                            scale=1.0,
                            accum_out=squares[:, g, b, n : n + 1],
                        )
                    for c in range(PIXELS // SUM_COLS):
                        nc.tensor.matmul(
                            out=sum_banks[g][:],
                            lhsT=ident[:],
                            rhs=x_sb[g][n][BY_SCALAR][:, :, c * SUM_COLS : (c + 1) * SUM_COLS],
                            start=(n == 0 and c == 0),
                            stop=(n == IMAGES - 1 and c == PIXELS // SUM_COLS - 1),
                        )
                    if g > 0 and n == CLOSE_IMAGE:
                        close_pass(g - 1)

            bias_ps = stat_banks.tile([P, P], BF16, name="bias_ps")
            nc.tensor.transpose(bias_ps[:], bias_rows[:], ident[:])
            nc.vector.tensor_copy(out=bias_col[:], in_=bias_ps[:, 0:O_TILES])

            close_pass(PASSES - 1)

            def deviation(a):
                nc.scalar.activation(
                    out=rstd[a][:], in_=var[a], func=ACT.Abs_reciprocal_sqrt, bias=EPS, scale=1.0
                )

            deviation(BY_VECTOR)
            def small(name):
                return stat.tile([P, PASSES, HALF], F32, name=name)

            early_squares = small("early_squares")
            nc.gpsimd.tensor_add(out=early_squares[:], in0=squares[:, :, :, 0], in1=squares[:, :, :, 1])
            for n in range(2, IMAGES - 1):
                nc.gpsimd.tensor_add(out=early_squares[:], in0=early_squares[:], in1=squares[:, :, :, n])
            early_mean_sq = small("early_mean_sq")
            nc.gpsimd.tensor_scalar(
                out=early_mean_sq[:], in0=early_squares[:], scalar1=1.0 / SAMPLES, scalar2=0.0, op0=ALU.mult, op1=ALU.add
            )
            nc.gpsimd.tensor_scalar(
                out=mean[BY_SCALAR], in0=sums[:], scalar1=1.0 / SAMPLES, scalar2=0.0, op0=ALU.mult, op1=ALU.add
            )
            offset = small("offset")
            nc.gpsimd.tensor_add(out=offset[:], in0=mean[BY_SCALAR], in1=neg_shift[:])
            offset_sq = small("offset_sq")
            nc.gpsimd.tensor_mul(out=offset_sq[:], in0=offset[:], in1=offset[:])
            var_rest = small("var_rest")
            nc.gpsimd.tensor_sub(out=var_rest[:], in0=early_mean_sq[:], in1=offset_sq[:])
            nc.vector.scalar_tensor_tensor(
                out=var[BY_SCALAR],
                in0=squares[:, :, :, IMAGES - 1],
                scalar=1.0 / SAMPLES,
                in1=var_rest[:],
                op0=ALU.mult,
                op1=ALU.add,
            )
            deviation(BY_SCALAR)

        def normalise(xn, n, g, a, cols):
            for b in range(HALF):
                nc.vector.tensor_scalar(
                    out=xn[:, a * HALF + b, cols],
                    in0=x_sb[g][n][a][:, b, cols],
                    scalar1=mean[a][:, g, b : b + 1],
                    scalar2=rstd[a][:, g, b : b + 1],
                    op0=ALU.subtract,
                    op1=ALU.mult,
                )

        def regroup(xn, col, width, copy):
            grouped = work.tile([P, N_TILE, PACK], BF16, name="grouped", align_bytes=256)
            copy(
                out=grouped[:, :width, :].rearrange("p (c i) t -> p c t i", i=RUN),
                in_=xn[:, :, col : col + width].rearrange("p t (c i) -> p c t i", i=RUN),
            )
            return grouped

        def quantise(grouped, width):
            codes = quant.tile([P, N_TILE], U32, name="codes", align_bytes=256)
            plane = quant.tile([P, N_TILE], U8, name="plane", align_bytes=256)
            nc.vector.quantize_mx(
                out=codes[:, :width].bitcast(FP8X4),
                scales=plane[:, :width],
                in_=grouped[:, :width, :].rearrange("p c t -> p (c t)"),
            )
            return codes, plane

        with tc.psum_pool(name="acc_banks", bufs=O_TILES) as acc_banks:

            def multiply(acc, o, g, codes, plane, width):
                o_cols = slice(o * P, (o + 1) * P)
                nc.tensor.matmul_mx(
                    out=acc[:, :width],
                    lhsT=w_words[:, g, o_cols].bitcast(FP8X4),
                    lhsT_scale=w_planes[:, g, o_cols],
                    rhs=codes[:, :width].bitcast(FP8X4),
                    rhs_scale=plane[:, :width],
                    start=(g == 0),
                    stop=(g == PASSES - 1),
                )

            def add_bias(result, acc, o, first, width):
                part = result[:, o % O_STORE, :width]
                if o in vector_banks(first, width):
                    nc.vector.tensor_scalar(
                        out=part, in0=acc[:, :width], scalar1=bias_col[:, o : o + 1], scalar2=None, op0=ALU.add
                    )
                else:
                    nc.scalar.activation(
                        out=part, in_=acc[:, :width], func=ACT.Identity, bias=bias_col[:, o : o + 1], scale=1.0
                    )

            def store(result, o, first, width):
                n, col = divmod(first, PIXELS)
                nc.sync.dma_start(
                    out=out_view[n, :, o - O_STORE + 1 : o + 1, col : col + width], in_=result[:, :, :width]
                )

            units = [(first, width, g) for first, width in pixel_tiles() for g in range(PASSES)]
            xn_of_pass = [None] * PASSES
            operands = [None] * PASSES

            def prepare(first, width, g):
                n, col = divmod(first, PIXELS)
                if first == 0:
                    if g == 0:
                        for h in range(PASSES):
                            xn_of_pass[h] = images.tile([P, PACK, PIXELS], BF16, name="xn")
                        for a in (BY_VECTOR, BY_SCALAR):
                            for h in range(PASSES):
                                normalise(xn_of_pass[h], n, h, a, slice(0, FIRST_NORMALISED))
                elif first == FIRST_NORMALISED or col == 0:
                    if col == 0:
                        xn_of_pass[g] = images.tile([P, PACK, PIXELS], BF16, name="xn")
                    for a in (BY_VECTOR, BY_SCALAR):
                        normalise(xn_of_pass[g], n, g, a, slice(col, PIXELS))
                by_scalar = g == 0 and width < N_TILE
                return regroup(xn_of_pass[g], col, width, nc.scalar.copy if by_scalar else nc.vector.tensor_copy)

            grouped_next = prepare(*units[0])
            for u, (first, width, g) in enumerate(units):
                grouped = grouped_next
                if u + 1 < len(units):
                    grouped_next = prepare(*units[u + 1])
                operands[g] = quantise(grouped, width)
                if g == PASSES - 1:
                    for o in range(O_TILES):
                        acc = acc_banks.tile([P, N_TILE], F32, name="acc")
                        for h, (codes, plane) in enumerate(operands):
                            multiply(acc, o, h, codes, plane, width)
                        if o % O_STORE == 0:
                            result = results.tile([P, O_STORE, N_TILE], F32, name="result")
                        add_bias(result, acc, o, first, width)
                        if o % O_STORE == O_STORE - 1:
                            store(result, o, first, width)
